import numpy as np
import ml_dtypes


BF16 = ml_dtypes.bfloat16


def bf(x):
    return np.asarray(x, np.float32).astype(BF16)


def f64(x):
    return np.asarray(x).astype(np.float64)


E2M1 = np.array([0.0, 0.5, 1.0, 1.5, 2.0, 3.0, 4.0, 6.0, -0.0, -0.5, -1.0, -1.5, -2.0, -3.0, -4.0, -6.0])


def pack_weight(w, fmt):
    k, n = w.shape
    w = f64(bf(w)).reshape(k // 32, 32, n)
    amax = np.abs(w).max(1)
    if fmt == "e4m3":
        byte = np.frexp(amax)[1] - 1 + 127 - 7
    else:
        mant, ex = np.frexp(amax / 6.0)
        byte = np.where(mant > 0.5, ex, ex - 1) + 127
    byte = np.clip(np.where(amax > 0, byte, 1), 1, 254)
    scaled = (w * np.exp2(127.0 - byte)[:, None, :]).reshape(k, n).astype(np.float32)
    by_word = np.ascontiguousarray(scaled.reshape(k // 512, 128, 4, n).transpose(0, 1, 3, 2))
    if fmt == "e4m3":
        words = by_word.astype(ml_dtypes.float8_e4m3fn).view(np.uint8)
    else:
        c = by_word.astype(ml_dtypes.float4_e2m1fn).view(np.uint8) & 0xF
        words = c[..., 0::2] | (c[..., 1::2] << 4)
    return np.ascontiguousarray(words), np.ascontiguousarray(byte.astype(np.uint8).reshape(k // 512, 16, n))


def unpack_weight(words, scales, fmt):
    g, p, n, _ = words.shape
    if fmt == "e4m3":
        vals = np.ascontiguousarray(words).view(ml_dtypes.float8_e4m3fn).astype(np.float64)
    else:
        nib = np.empty((g, p, n, 4), np.uint8)
        nib[..., 0::2] = words & 0xF
        nib[..., 1::2] = words >> 4
        vals = E2M1[nib]
    vals = vals * np.repeat(np.exp2(scales.astype(np.float64) - 127.0), 8, axis=1)[..., None]
    return vals.transpose(0, 1, 3, 2).reshape(g * 512, n)

def pack4(w):
    words, scales = pack_weight(w, "e2m1")
    return words.reshape(words.shape[0], 128, -1), scales


def unpack4(words, scales):
    return unpack_weight(words.reshape(words.shape[0], 128, -1, 2), scales, "e2m1")


def kspread(k):
    return np.exp2(np.repeat(np.random.randint(-6, 7, k // 32), 32).astype(np.float64))


B, S, D, H, KV, HD = 1, 512, 3072, 16, 4, 128
THETA = 10000.0
HALF = HD // 2


def rope_tables():
    inv_freq = 1.0 / (THETA ** (f64(np.arange(0, HD, 2)) / HD))
    ang = f64(np.arange(S))[:, None] * inv_freq[None, :]
    emb = np.concatenate([ang, ang], axis=-1)
    return np.cos(emb), np.sin(emb)


def rotate_half(t):
    return np.concatenate([-t[..., HALF:], t[..., :HALF]], axis=-1)


def apply_rope(t, cos, sin):
    return t * cos[None, None] + rotate_half(t) * sin[None, None]


def setup_inputs():
    s = kspread(D)
    w = 1.0 / np.sqrt(D)
    x = np.random.standard_normal((B, S, D)) * s
    x_words, x_scales = pack4(x.reshape(B * S, D).T)
    wq_words, wq_scales = pack4((np.random.standard_normal((H * HD, D)) * w / s[None, :]).T)
    wk_words, wk_scales = pack4((np.random.standard_normal((KV * HD, D)) * w / s[None, :]).T)
    wv_words, wv_scales = pack4((np.random.standard_normal((KV * HD, D)) * w / s[None, :]).T)
    return {"x_words": x_words, "x_scales": x_scales,
            "wq_words": wq_words, "wq_scales": wq_scales,
            "wk_words": wk_words, "wk_scales": wk_scales,
            "wv_words": wv_words, "wv_scales": wv_scales}


def reference(x_words, x_scales, wq_words, wq_scales, wk_words, wk_scales, wv_words, wv_scales):
    xq = unpack4(x_words, x_scales).T.reshape(B, S, D)
    q = (xq @ unpack4(wq_words, wq_scales)).reshape(B, S, H, HD).transpose(0, 2, 1, 3)
    k = (xq @ unpack4(wk_words, wk_scales)).reshape(B, S, KV, HD).transpose(0, 2, 1, 3)
    v = (xq @ unpack4(wv_words, wv_scales)).reshape(B, S, KV, HD).transpose(0, 2, 1, 3)
    cos, sin = rope_tables()
    return apply_rope(q, cos, sin), apply_rope(k, cos, sin), v

@@ -1,0 +1,215 @@
+import math
+from contextlib import ExitStack
+
+import concourse.mybir as mybir
+
+S, D, H, KV, HD = 512, 3072, 16, 4, 128
+THETA = 10000.0
+
+P = 128
+G = D // 512
+TB = S // P
+HALF = HD // 2
+NB = 512
+HPB = NB // HD
+QB = H * HD // NB
+
+FLOPS = 2 * S * D * (H + 2 * KV) * HD
+
+F32 = mybir.dt.float32
+I32 = mybir.dt.int32
+U8 = mybir.dt.uint8
+FP4X4 = mybir.dt.float4_e2m1fn_x4
+ALU = mybir.AluOpType
+ACT = mybir.ActivationFunctionType
+
+
+def tile_advancedattn_pa_kernel(
+    tc,
+    x_words,
+    x_scales,
+    wq_words,
+    wq_scales,
+    wk_words,
+    wk_scales,
+    wv_words,
+    wv_scales,
+    out_q,
+    out_k,
+    out_v,
+):
+    nc = tc.nc
+    with ExitStack() as ctx:
+        keep = ctx.enter_context(tc.tile_pool(name="keep", bufs=1))
+        work = ctx.enter_context(tc.tile_pool(name="work", bufs=4))
+        psum = ctx.enter_context(tc.psum_pool(name="psum", bufs=8))
+        ctx.enter_context(tc.manual_schedule())
+
+        def codes_tile(name):
+            return keep.tile([P, G, 2 * NB], U8, name=name, align_bytes=64)
+
+        def plane_tile(name, cols):
+            return keep.tile([P, G, cols], U8, name=name, align_bytes=64)
+
+        def load_codes(tile, words, g0, g1, c0):
+            nc.sync.dma_start(
+                out=tile[:, g0:g1, :].bitcast(I32),
+                in_=words[g0:g1, :, c0 : c0 + 2 * NB].rearrange("g p c -> p g c").bitcast(I32),
+            )
+
+        def load_scales(plane, scales, c0, cols):
+            for quad in range(4):
+                nc.sync.dma_start(
+                    out=plane[32 * quad : 32 * quad + 4, :, :].bitcast(I32),
+                    in_=scales[:, 4 * quad : 4 * quad + 4, c0 : c0 + cols]
+                    .rearrange("g r n -> r g n")
+                    .bitcast(I32),
+                )
+
+        def zero(engine, plane):
+            engine.memset(plane[:].rearrange("p g n -> p (g n)").bitcast(I32), 0)
+
+        x_codes = codes_tile("x_codes")
+        k_codes = codes_tile("k_codes")
+        v_codes = codes_tile("v_codes")
+        q_codes = [codes_tile(f"q_codes{n}") for n in range(QB)]
+        x_plane = plane_tile("x_plane", S)
+        k_plane = plane_tile("k_plane", NB)
+        v_plane = plane_tile("v_plane", NB)
+        q_planes = [plane_tile(f"q_plane{i}", 2 * NB) for i in range(QB // 2)]
+
+        zero(nc.vector, x_plane)
+        zero(nc.gpsimd, k_plane)
+
+        load_codes(x_codes, x_words, 0, 1, 0)
+        load_codes(k_codes, wk_words, 0, 1, 0)
+        load_scales(x_plane, x_scales, 0, S)
+        load_scales(k_plane, wk_scales, 0, NB)
+        for g0, g1 in ((1, 2), (2, 4), (4, 6)):
+            load_codes(x_codes, x_words, g0, g1, 0)
+            load_codes(k_codes, wk_words, g0, g1, 0)
+
+        pos = keep.tile([P, TB], F32, name="pos")
+        nc.gpsimd.iota(
+            pos[:], pattern=[[P, TB]], base=0, channel_multiplier=1, allow_small_or_imprecise_dtypes=True
+        )
+        for plane in q_planes:
+            zero(nc.gpsimd, plane)
+        zero(nc.gpsimd, v_plane)
+
+        for pair in range(QB // 2):
+            load_scales(q_planes[pair], wq_scales, 2 * NB * pair, 2 * NB)
+            for n in (2 * pair, 2 * pair + 1):
+                for g0, g1 in ((0, 3), (3, 6)):
+                    load_codes(q_codes[n], wq_words, g0, g1, 2 * NB * n)
+        load_scales(v_plane, wv_scales, 0, NB)
+        for g0, g1 in ((0, 3), (3, 6)):
+            load_codes(v_codes, wv_words, g0, g1, 0)
+
+        freq = keep.tile([P, HALF], F32, name="freq")
+        one = keep.tile([P, 1], F32, name="one")
+        warm = keep.tile([P, 1], F32, name="warm")
+        nc.vector.memset(one[:], 1.0)
+        nc.scalar.activation(out=warm[:], in_=one[:], func=ACT.Sin)
+        nc.vector.tensor_scalar(
+            out=freq[:, 0:1], in0=one[:], scalar1=1.0 / (2.0 * math.pi), scalar2=None, op0=ALU.mult
+        )
+        width = 1
+        while width < HALF:
+            nc.vector.tensor_scalar(
+                out=freq[:, width : 2 * width],
+                in0=freq[:, 0:width],
+                scalar1=THETA ** (-width / HALF),
+                scalar2=None,
+                op0=ALU.mult,
+            )
+            width *= 2
+        turns = keep.tile([P, 2, TB, HALF], F32, name="turns")
+        whole = keep.tile([P, 2, TB, HALF], I32, name="whole")
+        part = keep.tile([P, 2, TB, HALF], F32, name="part")
+        for b in range(TB):
+            nc.vector.tensor_scalar(
+                out=turns[:, 0, b, :], in0=freq[:], scalar1=pos[:, b : b + 1], scalar2=None, op0=ALU.mult
+            )
+        nc.vector.tensor_scalar(
+            out=turns[:, 1, :, :], in0=turns[:, 0, :, :], scalar1=0.25, scalar2=None, op0=ALU.add
+        )
+        nc.vector.tensor_copy(out=whole[:], in_=turns[:])
+        nc.vector.tensor_tensor(out=part[:], in0=turns[:], in1=whole[:], op=ALU.subtract)
+        cos = keep.tile([P, TB, HALF], F32, name="cos")
+        sin = keep.tile([P, TB, 2, HALF], F32, name="sin")
+        nc.scalar.activation(out=cos[:], in_=part[:, 1, :, :], func=ACT.Sin, scale=2.0 * math.pi)
+        nc.scalar.activation(out=sin[:, :, 0, :], in_=part[:, 0, :, :], func=ACT.Sin, scale=-2.0 * math.pi)
+        nc.scalar.activation(out=sin[:, :, 1, :], in_=part[:, 0, :, :], func=ACT.Sin, scale=2.0 * math.pi)
+
+        def multiply(acc, tb, g, codes, plane, c0, n0, cols):
+            nc.tensor.matmul_mx(
+                out=acc,
+                lhsT=x_codes[:, g, 2 * P * tb : 2 * P * (tb + 1)].bitcast(FP4X4),
+                lhsT_scale=x_plane[:, g, P * tb : P * (tb + 1)],
+                rhs=codes[:, g, 2 * c0 : 2 * (c0 + cols)].bitcast(FP4X4),
+                rhs_scale=plane[:, g, n0 + c0 : n0 + c0 + cols],
+                start=(g == 0),
+                stop=(g == G - 1),
+            )
+
+        def heads(out, h0, h1, tb):
+            return out[0, h0:h1, P * tb : P * (tb + 1), :].rearrange("h p j -> p h j")
+
+        def rope_and_store(acc, tb, out, h0):
+            res = work.tile([P, NB], F32, name="res", bufs=6)
+            rot = work.tile([P, NB], F32, name="rot")
+            nc.vector.tensor_tensor(
+                out=res[:].rearrange("p (h j) -> p h j", j=HALF),
+                in0=acc[:].rearrange("p (h j) -> p h j", j=HALF),
+                in1=cos[:, tb, :].unsqueeze(1).to_broadcast([P, 2 * HPB, HALF]),
+                op=ALU.mult,
+            )
+            nc.vector.tensor_tensor(
+                out=rot[:].rearrange("p (h s j) -> p h s j", s=2, j=HALF),
+                in0=acc[:].rearrange("p (h s j) -> p h s j", s=2, j=HALF)[:, :, ::-1, :],
+                in1=sin[:, tb, :, :].unsqueeze(1).to_broadcast([P, HPB, 2, HALF]),
+                op=ALU.mult,
+            )
+            nc.gpsimd.tensor_tensor(out=res[:], in0=res[:], in1=rot[:], op=ALU.add)
+            nc.sync.dma_start(
+                out=heads(out, h0, h0 + HPB, tb), in_=res[:].rearrange("p (h j) -> p h j", j=HD)
+            )
+
+        accs = [psum.tile([P, NB], F32, name="acc") for b in range(TB)]
+        for g in range(G):
+            for tb in range(TB):
+                multiply(accs[tb][:], tb, g, k_codes, k_plane, 0, 0, NB)
+        for tb in range(TB):
+            rope_and_store(accs[tb], tb, out_k, 0)
+
+        for n in range(QB):
+            for tb in range(TB):
+                acc = psum.tile([P, NB], F32, name="acc")
+                for g in range(G):
+                    multiply(acc[:], tb, g, q_codes[n], q_planes[n // 2], 0, NB * (n % 2), NB)
+                rope_and_store(acc, tb, out_q, HPB * n)
+
+        for tb in range(TB - 1):
+            acc = psum.tile([P, NB], F32, name="acc")
+            for g in range(G):
+                multiply(acc[:], tb, g, v_codes, v_plane, 0, 0, NB)
+            res = work.tile([P, NB], F32, name="res", bufs=6)
+            nc.scalar.copy(out=res[:], in_=acc[:])
+            nc.sync.dma_start(out=heads(out_v, 0, HPB, tb), in_=res[:].rearrange("p (h j) -> p h j", j=HD))
+
+        tb = TB - 1
+        for half in range(2):
+            cols = NB // 2
+            acc = psum.tile([P, NB], F32, name="acc")
+            for g in range(G):
+                multiply(acc[:, 0:cols], tb, g, v_codes, v_plane, cols * half, 0, cols)
+            res = work.tile([P, NB], F32, name="res", bufs=6)
+            if half == 0:
+                nc.scalar.copy(out=res[:, 0:cols], in_=acc[:, 0:cols])
+            else:
+                nc.vector.tensor_copy(out=res[:, 0:cols], in_=acc[:, 0:cols])
+            nc.sync.dma_start(
+                out=heads(out_v, half * HPB // 2, (half + 1) * HPB // 2, tb),
+                in_=res[:, 0:cols].rearrange("p (h j) -> p h j", j=HD),
+            )

@@ -8,6 +8,7 @@ THETA = 10000.0
 
 P = 128
 G = D // 512
+G2 = G // 2
 TB = S // P
 HALF = HD // 2
 NB = 512
@@ -17,6 +18,7 @@ QB = H * HD // NB
 FLOPS = 2 * S * D * (H + 2 * KV) * HD
 
 F32 = mybir.dt.float32
+BF16 = mybir.dt.bfloat16
 I32 = mybir.dt.int32
 U8 = mybir.dt.uint8
 FP4X4 = mybir.dt.float4_e2m1fn_x4
@@ -48,8 +50,8 @@ def tile_advancedattn_pa_kernel(
         def codes_tile(name):
             return keep.tile([P, G, 2 * NB], U8, name=name, align_bytes=64)
 
-        def plane_tile(name, cols):
-            return keep.tile([P, G, cols], U8, name=name, align_bytes=64)
+        def plane_tile(name):
+            return keep.tile([P, G, NB], U8, name=name, align_bytes=64)
 
         def load_codes(tile, words, g0, g1, c0):
             nc.sync.dma_start(
@@ -57,54 +59,59 @@ def tile_advancedattn_pa_kernel(
                 in_=words[g0:g1, :, c0 : c0 + 2 * NB].rearrange("g p c -> p g c").bitcast(I32),
             )
 
-        def load_scales(plane, scales, c0, cols):
+        def load_scales(plane, scales, g0, g1, c0):
             for quad in range(4):
                 nc.sync.dma_start(
-                    out=plane[32 * quad : 32 * quad + 4, :, :].bitcast(I32),
-                    in_=scales[:, 4 * quad : 4 * quad + 4, c0 : c0 + cols]
+                    out=plane[32 * quad : 32 * quad + 4, g0:g1, :].bitcast(I32),
+                    in_=scales[g0:g1, 4 * quad : 4 * quad + 4, c0 : c0 + NB]
                     .rearrange("g r n -> r g n")
                     .bitcast(I32),
                 )
 
-        def zero(engine, plane):
-            engine.memset(plane[:].rearrange("p g n -> p (g n)").bitcast(I32), 0)
+        def zero(engine, plane, g0, g1):
+            engine.memset(plane[:, g0:g1, :].rearrange("p g n -> p (g n)").bitcast(I32), 0)
 
         x_codes = codes_tile("x_codes")
         k_codes = codes_tile("k_codes")
         v_codes = codes_tile("v_codes")
         q_codes = [codes_tile(f"q_codes{n}") for n in range(QB)]
-        x_plane = plane_tile("x_plane", S)
-        k_plane = plane_tile("k_plane", NB)
-        v_plane = plane_tile("v_plane", NB)
-        q_planes = [plane_tile(f"q_plane{i}", 2 * NB) for i in range(QB // 2)]
+        x_plane = plane_tile("x_plane")
+        k_plane = plane_tile("k_plane")
+        v_plane = plane_tile("v_plane")
+        q_planes = [plane_tile(f"q_plane{n}") for n in range(QB)]
 
-        zero(nc.vector, x_plane)
-        zero(nc.gpsimd, k_plane)
-
-        load_codes(x_codes, x_words, 0, 1, 0)
-        load_codes(k_codes, wk_words, 0, 1, 0)
-        load_scales(x_plane, x_scales, 0, S)
-        load_scales(k_plane, wk_scales, 0, NB)
-        for g0, g1 in ((1, 2), (2, 4), (4, 6)):
-            load_codes(x_codes, x_words, g0, g1, 0)
-            load_codes(k_codes, wk_words, g0, g1, 0)
-
+        zero(nc.vector, x_plane, 0, G2)
+        zero(nc.gpsimd, k_plane, 0, G2)
+        dummy = keep.tile([P, NB], BF16, name="dummy")
+        nc.vector.memset(dummy[:], 0.0)
+        zero(nc.vector, x_plane, G2, G)
+        zero(nc.gpsimd, v_plane, 0, G)
+        zero(nc.gpsimd, k_plane, G2, G)
         pos = keep.tile([P, TB], F32, name="pos")
         nc.gpsimd.iota(
             pos[:], pattern=[[P, TB]], base=0, channel_multiplier=1, allow_small_or_imprecise_dtypes=True
         )
         for plane in q_planes:
-            zero(nc.gpsimd, plane)
-        zero(nc.gpsimd, v_plane)
+            zero(nc.gpsimd, plane, 0, G)
 
-        for pair in range(QB // 2):
-            load_scales(q_planes[pair], wq_scales, 2 * NB * pair, 2 * NB)
-            for n in (2 * pair, 2 * pair + 1):
-                for g0, g1 in ((0, 3), (3, 6)):
-                    load_codes(q_codes[n], wq_words, g0, g1, 2 * NB * n)
-        load_scales(v_plane, wv_scales, 0, NB)
-        for g0, g1 in ((0, 3), (3, 6)):
-            load_codes(v_codes, wv_words, g0, g1, 0)
+        load_codes(x_codes, x_words, 0, 1, 0)
+        load_codes(k_codes, wk_words, 0, 1, 0)
+        load_scales(x_plane, x_scales, 0, G2, 0)
+        load_scales(k_plane, wk_scales, 0, G2, 0)
+        for g in range(1, G2):
+            load_codes(x_codes, x_words, g, g + 1, 0)
+            load_codes(k_codes, wk_words, g, g + 1, 0)
+        load_scales(v_plane, wv_scales, 0, G, 0)
+        load_codes(v_codes, wv_words, 0, G2, 0)
+        load_scales(x_plane, x_scales, G2, G, 0)
+        load_codes(x_codes, x_words, G2, G, 0)
+        load_codes(v_codes, wv_words, G2, G, 0)
+        load_scales(k_plane, wk_scales, G2, G, 0)
+        load_codes(k_codes, wk_words, G2, G, 0)
+        for n in range(QB):
+            load_scales(q_planes[n], wq_scales, 0, G, NB * n)
+            load_codes(q_codes[n], wq_words, 0, G2, 2 * NB * n)
+            load_codes(q_codes[n], wq_words, G2, G, 2 * NB * n)
 
         freq = keep.tile([P, HALF], F32, name="freq")
         one = keep.tile([P, 1], F32, name="one")
@@ -142,13 +149,13 @@ def tile_advancedattn_pa_kernel(
         nc.scalar.activation(out=sin[:, :, 0, :], in_=part[:, 0, :, :], func=ACT.Sin, scale=-2.0 * math.pi)
         nc.scalar.activation(out=sin[:, :, 1, :], in_=part[:, 0, :, :], func=ACT.Sin, scale=2.0 * math.pi)
 
-        def multiply(acc, tb, g, codes, plane, c0, n0, cols):
+        def multiply(acc, tb, g, codes, plane, c0, cols):
             nc.tensor.matmul_mx(
                 out=acc,
                 lhsT=x_codes[:, g, 2 * P * tb : 2 * P * (tb + 1)].bitcast(FP4X4),
                 lhsT_scale=x_plane[:, g, P * tb : P * (tb + 1)],
                 rhs=codes[:, g, 2 * c0 : 2 * (c0 + cols)].bitcast(FP4X4),
-                rhs_scale=plane[:, g, n0 + c0 : n0 + c0 + cols],
+                rhs_scale=plane[:, g, c0 : c0 + cols],
                 start=(g == 0),
                 stop=(g == G - 1),
             )
@@ -156,8 +163,8 @@ def tile_advancedattn_pa_kernel(
         def heads(out, h0, h1, tb):
             return out[0, h0:h1, P * tb : P * (tb + 1), :].rearrange("h p j -> p h j")
 
-        def rope_and_store(acc, tb, out, h0):
-            res = work.tile([P, NB], F32, name="res", bufs=6)
+        def rope_and_store(acc, tb, out, h0, adder):
+            res = work.tile([P, NB], F32, name="res", bufs=8)
             rot = work.tile([P, NB], F32, name="rot")
             nc.vector.tensor_tensor(
                 out=res[:].rearrange("p (h j) -> p h j", j=HALF),
@@ -171,40 +178,45 @@ def tile_advancedattn_pa_kernel(
                 in1=sin[:, tb, :, :].unsqueeze(1).to_broadcast([P, HPB, 2, HALF]),
                 op=ALU.mult,
             )
-            nc.gpsimd.tensor_tensor(out=res[:], in0=res[:], in1=rot[:], op=ALU.add)
+            adder.tensor_tensor(out=res[:], in0=res[:], in1=rot[:], op=ALU.add)
             nc.sync.dma_start(
                 out=heads(out, h0, h0 + HPB, tb), in_=res[:].rearrange("p (h j) -> p h j", j=HD)
             )
 
-        accs = [psum.tile([P, NB], F32, name="acc") for b in range(TB)]
-        for g in range(G):
-            for tb in range(TB):
-                multiply(accs[tb][:], tb, g, k_codes, k_plane, 0, 0, NB)
+        scratch = psum.tile([P, NB], F32, name="acc")
+        for i in range(10):
+            nc.tensor.matmul(scratch[:], lhsT=dummy[:, 0:P], rhs=dummy[:], start=True, stop=True)
+
+        k_accs = [psum.tile([P, NB], F32, name="acc") for b in range(TB)]
+        v_accs = [psum.tile([P, NB], F32, name="acc") for b in range(TB - 1)]
+        k_group = (k_accs, k_codes, k_plane)
+        v_group = (v_accs, v_codes, v_plane)
+        for g0, groups in ((0, (k_group, v_group)), (G2, (v_group, k_group))):
+            for accs, codes, plane in groups:
+                for g in range(g0, g0 + G2):
+                    for tb in range(len(accs)):
+                        multiply(accs[tb][:], tb, g, codes, plane, 0, NB)
+        for tb in range(TB - 1):
+            res = work.tile([P, NB], F32, name="res", bufs=8)
+            nc.scalar.copy(out=res[:], in_=v_accs[tb][:])
+            nc.sync.dma_start(out=heads(out_v, 0, HPB, tb), in_=res[:].rearrange("p (h j) -> p h j", j=HD))
         for tb in range(TB):
-            rope_and_store(accs[tb], tb, out_k, 0)
+            rope_and_store(k_accs[tb], tb, out_k, 0, nc.gpsimd)
 
         for n in range(QB):
             for tb in range(TB):
                 acc = psum.tile([P, NB], F32, name="acc")
                 for g in range(G):
-                    multiply(acc[:], tb, g, q_codes[n], q_planes[n // 2], 0, NB * (n % 2), NB)
-                rope_and_store(acc, tb, out_q, HPB * n)
-
-        for tb in range(TB - 1):
-            acc = psum.tile([P, NB], F32, name="acc")
-            for g in range(G):
-                multiply(acc[:], tb, g, v_codes, v_plane, 0, 0, NB)
-            res = work.tile([P, NB], F32, name="res", bufs=6)
-            nc.scalar.copy(out=res[:], in_=acc[:])
-            nc.sync.dma_start(out=heads(out_v, 0, HPB, tb), in_=res[:].rearrange("p (h j) -> p h j", j=HD))
+                    multiply(acc[:], tb, g, q_codes[n], q_planes[n], 0, NB)
+                rope_and_store(acc, tb, out_q, HPB * n, nc.vector if n == QB - 1 and tb > 0 else nc.gpsimd)
 
         tb = TB - 1
         for half in range(2):
             cols = NB // 2
             acc = psum.tile([P, NB], F32, name="acc")
             for g in range(G):
-                multiply(acc[:, 0:cols], tb, g, v_codes, v_plane, cols * half, 0, cols)
-            res = work.tile([P, NB], F32, name="res", bufs=6)
+                multiply(acc[:, 0:cols], tb, g, v_codes, v_plane, cols * half, cols)
+            res = work.tile([P, NB], F32, name="res", bufs=8)
             if half == 0:
                 nc.scalar.copy(out=res[:, 0:cols], in_=acc[:, 0:cols])
             else:

@@ -103,11 +103,11 @@ def tile_advancedattn_pa_kernel(
             load_codes(k_codes, wk_words, g, g + 1, 0)
         load_scales(v_plane, wv_scales, 0, G, 0)
         load_codes(v_codes, wv_words, 0, G2, 0)
-        load_scales(x_plane, x_scales, G2, G, 0)
         load_codes(x_codes, x_words, G2, G, 0)
-        load_codes(v_codes, wv_words, G2, G, 0)
-        load_scales(k_plane, wk_scales, G2, G, 0)
         load_codes(k_codes, wk_words, G2, G, 0)
+        load_scales(x_plane, x_scales, G2, G, 0)
+        load_scales(k_plane, wk_scales, G2, G, 0)
+        load_codes(v_codes, wv_words, G2, G, 0)
         for n in range(QB):
             load_scales(q_planes[n], wq_scales, 0, G, NB * n)
             load_codes(q_codes[n], wq_words, 0, G2, 2 * NB * n)
@@ -163,7 +163,18 @@ def tile_advancedattn_pa_kernel(
         def heads(out, h0, h1, tb):
             return out[0, h0:h1, P * tb : P * (tb + 1), :].rearrange("h p j -> p h j")
 
-        def rope_and_store(acc, tb, out, h0, adder):
+        waiting = []
+
+        def add_and_store(engine, res, rot, dst):
+            engine.tensor_tensor(out=res[:], in0=res[:], in1=rot[:], op=ALU.add)
+            nc.sync.dma_start(out=dst, in_=res[:].rearrange("p (h j) -> p h j", j=HD))
+
+        def flush():
+            while len(waiting) > 0:
+                add_and_store(nc.vector, *waiting[0])
+                waiting.remove(waiting[0])
+
+        def rope(acc, tb, out, h0, on_gpsimd):
             res = work.tile([P, NB], F32, name="res", bufs=8)
             rot = work.tile([P, NB], F32, name="rot")
             nc.vector.tensor_tensor(
@@ -172,16 +183,18 @@ def tile_advancedattn_pa_kernel(
                 in1=cos[:, tb, :].unsqueeze(1).to_broadcast([P, 2 * HPB, HALF]),
                 op=ALU.mult,
             )
+            flush()
             nc.vector.tensor_tensor(
                 out=rot[:].rearrange("p (h s j) -> p h s j", s=2, j=HALF),
                 in0=acc[:].rearrange("p (h s j) -> p h s j", s=2, j=HALF)[:, :, ::-1, :],
                 in1=sin[:, tb, :, :].unsqueeze(1).to_broadcast([P, HPB, 2, HALF]),
                 op=ALU.mult,
             )
-            adder.tensor_tensor(out=res[:], in0=res[:], in1=rot[:], op=ALU.add)
-            nc.sync.dma_start(
-                out=heads(out, h0, h0 + HPB, tb), in_=res[:].rearrange("p (h j) -> p h j", j=HD)
-            )
+            dst = heads(out, h0, h0 + HPB, tb)
+            if on_gpsimd:
+                add_and_store(nc.gpsimd, res, rot, dst)
+            else:
+                waiting.append((res, rot, dst))
 
         scratch = psum.tile([P, NB], F32, name="acc")
         for i in range(10):
@@ -191,24 +204,25 @@ def tile_advancedattn_pa_kernel(
         v_accs = [psum.tile([P, NB], F32, name="acc") for b in range(TB - 1)]
         k_group = (k_accs, k_codes, k_plane)
         v_group = (v_accs, v_codes, v_plane)
-        for g0, groups in ((0, (k_group, v_group)), (G2, (v_group, k_group))):
+        for g0, groups in ((0, (k_group, v_group)), (G2, (k_group, v_group))):
             for accs, codes, plane in groups:
                 for g in range(g0, g0 + G2):
                     for tb in range(len(accs)):
                         multiply(accs[tb][:], tb, g, codes, plane, 0, NB)
+        for tb in range(TB):
+            rope(k_accs[tb], tb, out_k, 0, True)
         for tb in range(TB - 1):
             res = work.tile([P, NB], F32, name="res", bufs=8)
             nc.scalar.copy(out=res[:], in_=v_accs[tb][:])
             nc.sync.dma_start(out=heads(out_v, 0, HPB, tb), in_=res[:].rearrange("p (h j) -> p h j", j=HD))
-        for tb in range(TB):
-            rope_and_store(k_accs[tb], tb, out_k, 0, nc.gpsimd)
 
         for n in range(QB):
             for tb in range(TB):
                 acc = psum.tile([P, NB], F32, name="acc")
                 for g in range(G):
                     multiply(acc[:], tb, g, q_codes[n], q_planes[n], 0, NB)
-                rope_and_store(acc, tb, out_q, HPB * n, nc.vector if n == QB - 1 and tb > 0 else nc.gpsimd)
+                rope(acc, tb, out_q, HPB * n, tb % 2 == 0)
+        flush()
 
         tb = TB - 1
         for half in range(2):
@@ -217,11 +231,8 @@ def tile_advancedattn_pa_kernel(
             for g in range(G):
                 multiply(acc[:, 0:cols], tb, g, v_codes, v_plane, cols * half, cols)
             res = work.tile([P, NB], F32, name="res", bufs=8)
-            if half == 0:
-                nc.scalar.copy(out=res[:, 0:cols], in_=acc[:, 0:cols])
-            else:
-                nc.vector.tensor_copy(out=res[:, 0:cols], in_=acc[:, 0:cols])
-            nc.sync.dma_start(
+            nc.scalar.copy(out=res[:, 0:cols], in_=acc[:, 0:cols])
+            nc.scalar.dma_start(
                 out=heads(out_v, half * HPB // 2, (half + 1) * HPB // 2, tb),
                 in_=res[:, 0:cols].rearrange("p (h j) -> p h j", j=HD),
             )

@@ -47,17 +47,27 @@ def tile_advancedattn_pa_kernel(
         psum = ctx.enter_context(tc.psum_pool(name="psum", bufs=8))
         ctx.enter_context(tc.manual_schedule())
 
-        def codes_tile(name):
-            return keep.tile([P, G, 2 * NB], U8, name=name, align_bytes=64)
+        def codes_tile(name, cols=NB):
+            return keep.tile([P, G, 2 * cols], U8, name=name, align_bytes=64)
 
-        def plane_tile(name):
-            return keep.tile([P, G, NB], U8, name=name, align_bytes=64)
+        def plane_tile(name, cols=NB):
+            return keep.tile([P, G, cols], U8, name=name, align_bytes=64)
 
         def load_codes(tile, words, g0, g1, c0):
+            width = tile.shape[2]
             nc.sync.dma_start(
                 out=tile[:, g0:g1, :].bitcast(I32),
-                in_=words[g0:g1, :, c0 : c0 + 2 * NB].rearrange("g p c -> p g c").bitcast(I32),
+                in_=words[g0:g1, :, c0 : c0 + width].rearrange("g p c -> p g c").bitcast(I32),
             )
+
+        def load_q_scales(pair, r):
+            nc.sync.dma_start(
+                out=q_planes[pair][r:P:32, :, :].bitcast(I32),
+                in_=wq_scales[:, r:16:4, 2 * NB * pair : 2 * NB * (pair + 1)].rearrange("g q n -> q g n").bitcast(I32),
+            )
+
+        def load_q_codes(pair, g0):
+            load_codes(q_codes[pair], wq_words, g0, g0 + 2, 4 * NB * pair)
 
         def load_scales(plane, scales, g0, g1, c0):
             for quad in range(4):
@@ -74,11 +84,11 @@ def tile_advancedattn_pa_kernel(
         x_codes = codes_tile("x_codes")
         k_codes = codes_tile("k_codes")
         v_codes = codes_tile("v_codes")
-        q_codes = [codes_tile(f"q_codes{n}") for n in range(QB)]
+        q_codes = [codes_tile(f"q_codes{i}", 2 * NB) for i in range(QB // 2)]
         x_plane = plane_tile("x_plane")
         k_plane = plane_tile("k_plane")
         v_plane = plane_tile("v_plane")
-        q_planes = [plane_tile(f"q_plane{n}") for n in range(QB)]
+        q_planes = [plane_tile(f"q_plane{i}", 2 * NB) for i in range(QB // 2)]
 
         zero(nc.vector, x_plane, 0, G2)
         zero(nc.gpsimd, k_plane, 0, G2)
@@ -106,12 +116,19 @@ def tile_advancedattn_pa_kernel(
         load_codes(x_codes, x_words, G2, G, 0)
         load_codes(k_codes, wk_words, G2, G, 0)
         load_scales(x_plane, x_scales, G2, G, 0)
+        load_q_scales(0, 0)
         load_scales(k_plane, wk_scales, G2, G, 0)
         load_codes(v_codes, wv_words, G2, G, 0)
-        for n in range(QB):
-            load_scales(q_planes[n], wq_scales, 0, G, NB * n)
-            load_codes(q_codes[n], wq_words, 0, G2, 2 * NB * n)
-            load_codes(q_codes[n], wq_words, G2, G, 2 * NB * n)
+        load_q_scales(0, 1)
+        load_q_codes(0, 0)
+        load_q_scales(0, 2)
+        load_q_codes(0, 2)
+        load_q_scales(0, 3)
+        load_q_codes(0, 4)
+        for i in range(3):
+            load_q_scales(1, i)
+            load_q_codes(1, 2 * i)
+        load_q_scales(1, 3)
 
         freq = keep.tile([P, HALF], F32, name="freq")
         one = keep.tile([P, 1], F32, name="one")
@@ -220,7 +237,7 @@ def tile_advancedattn_pa_kernel(
             for tb in range(TB):
                 acc = psum.tile([P, NB], F32, name="acc")
                 for g in range(G):
-                    multiply(acc[:], tb, g, q_codes[n], q_planes[n], 0, NB)
+                    multiply(acc[:], tb, g, q_codes[n // 2], q_planes[n // 2], NB * (n % 2), NB)
                 rope(acc, tb, out_q, HPB * n, tb % 2 == 0)
         flush()
 

@@ -113,15 +113,15 @@ def tile_advancedattn_pa_kernel(
             load_codes(k_codes, wk_words, g, g + 1, 0)
         load_scales(v_plane, wv_scales, 0, G, 0)
         load_codes(v_codes, wv_words, 0, G2, 0)
+        load_q_scales(0, 0)
         load_codes(x_codes, x_words, G2, G, 0)
         load_codes(k_codes, wk_words, G2, G, 0)
         load_scales(x_plane, x_scales, G2, G, 0)
-        load_q_scales(0, 0)
+        load_q_scales(0, 1)
         load_scales(k_plane, wk_scales, G2, G, 0)
         load_codes(v_codes, wv_words, G2, G, 0)
-        load_q_scales(0, 1)
-        load_q_codes(0, 0)
         load_q_scales(0, 2)
+        load_q_codes(0, 0)
         load_q_codes(0, 2)
         load_q_scales(0, 3)
         load_q_codes(0, 4)
@@ -183,31 +183,34 @@ def tile_advancedattn_pa_kernel(
         waiting = []
 
         def add_and_store(engine, res, rot, dst):
-            engine.tensor_tensor(out=res[:], in0=res[:], in1=rot[:], op=ALU.add)
-            nc.sync.dma_start(out=dst, in_=res[:].rearrange("p (h j) -> p h j", j=HD))
+            engine.tensor_tensor(out=res, in0=res, in1=rot, op=ALU.add)
+            nc.sync.dma_start(out=dst, in_=res.rearrange("p (h j) -> p h j", j=HD))
 
         def flush():
             while len(waiting) > 0:
                 add_and_store(nc.vector, *waiting[0])
                 waiting.remove(waiting[0])
 
-        def rope(acc, tb, out, h0, on_gpsimd):
-            res = work.tile([P, NB], F32, name="res", bufs=8)
-            rot = work.tile([P, NB], F32, name="rot")
+        def rope(acc, tb, out, h0, n_heads, on_gpsimd):
+            cols = n_heads * HD
+            res_tile = work.tile([P, NB], F32, name="res", bufs=8)
+            rot_tile = work.tile([P, NB], F32, name="rot")
+            res = res_tile[:, 0:cols]
+            rot = rot_tile[:, 0:cols]
             nc.vector.tensor_tensor(
-                out=res[:].rearrange("p (h j) -> p h j", j=HALF),
-                in0=acc[:].rearrange("p (h j) -> p h j", j=HALF),
-                in1=cos[:, tb, :].unsqueeze(1).to_broadcast([P, 2 * HPB, HALF]),
+                out=res.rearrange("p (h j) -> p h j", j=HALF),
+                in0=acc.rearrange("p (h j) -> p h j", j=HALF),
+                in1=cos[:, tb, :].unsqueeze(1).to_broadcast([P, 2 * n_heads, HALF]),
                 op=ALU.mult,
             )
             flush()
             nc.vector.tensor_tensor(
-                out=rot[:].rearrange("p (h s j) -> p h s j", s=2, j=HALF),
-                in0=acc[:].rearrange("p (h s j) -> p h s j", s=2, j=HALF)[:, :, ::-1, :],
-                in1=sin[:, tb, :, :].unsqueeze(1).to_broadcast([P, HPB, 2, HALF]),
+                out=rot.rearrange("p (h s j) -> p h s j", s=2, j=HALF),
+                in0=acc.rearrange("p (h s j) -> p h s j", s=2, j=HALF)[:, :, ::-1, :],
+                in1=sin[:, tb, :, :].unsqueeze(1).to_broadcast([P, n_heads, 2, HALF]),
                 op=ALU.mult,
             )
-            dst = heads(out, h0, h0 + HPB, tb)
+            dst = heads(out, h0, h0 + n_heads, tb)
             if on_gpsimd:
                 add_and_store(nc.gpsimd, res, rot, dst)
             else:
@@ -227,7 +230,7 @@ def tile_advancedattn_pa_kernel(
                     for tb in range(len(accs)):
                         multiply(accs[tb][:], tb, g, codes, plane, 0, NB)
         for tb in range(TB):
-            rope(k_accs[tb], tb, out_k, 0, True)
+            rope(k_accs[tb][:], tb, out_k, 0, HPB, True)
         for tb in range(TB - 1):
             res = work.tile([P, NB], F32, name="res", bufs=8)
             nc.scalar.copy(out=res[:], in_=v_accs[tb][:])
@@ -235,10 +238,14 @@ def tile_advancedattn_pa_kernel(
 
         for n in range(QB):
             for tb in range(TB):
-                acc = psum.tile([P, NB], F32, name="acc")
-                for g in range(G):
-                    multiply(acc[:], tb, g, q_codes[n // 2], q_planes[n // 2], NB * (n % 2), NB)
-                rope(acc, tb, out_q, HPB * n, tb % 2 == 0)
+                parts = 2 if n == QB - 1 and tb == TB - 1 else 1
+                cols = NB // parts
+                for i in range(parts):
+                    acc = psum.tile([P, NB], F32, name="acc")
+                    for g in range(G):
+                        multiply(acc[:, 0:cols], tb, g, q_codes[n // 2], q_planes[n // 2], NB * (n % 2) + cols * i, cols)
+                    h0 = HPB * n + cols // HD * i
+                    rope(acc[:, 0:cols], tb, out_q, h0, cols // HD, tb < TB - 1)
         flush()
 
         tb = TB - 1

import math
from contextlib import ExitStack

import concourse.mybir as mybir

S, D, H, KV, HD = 512, 3072, 16, 4, 128
THETA = 10000.0

P = 128
G = D // 512
G2 = G // 2
TB = S // P
HALF = HD // 2
NB = 512
HPB = NB // HD
QB = H * HD // NB

FLOPS = 2 * S * D * (H + 2 * KV) * HD

F32 = mybir.dt.float32
BF16 = mybir.dt.bfloat16
I32 = mybir.dt.int32
U8 = mybir.dt.uint8
FP4X4 = mybir.dt.float4_e2m1fn_x4
ALU = mybir.AluOpType
ACT = mybir.ActivationFunctionType


def tile_advancedattn_pa_kernel(
    tc,
    x_words,
    x_scales,
    wq_words,
    wq_scales,
    wk_words,
    wk_scales,
    wv_words,
    wv_scales,
    out_q,
    out_k,
    out_v,
):
    nc = tc.nc
    with ExitStack() as ctx:
        keep = ctx.enter_context(tc.tile_pool(name="keep", bufs=1))
        work = ctx.enter_context(tc.tile_pool(name="work", bufs=4))
        psum = ctx.enter_context(tc.psum_pool(name="psum", bufs=8))
        ctx.enter_context(tc.manual_schedule())

        def codes_tile(name, cols=NB):
            return keep.tile([P, G, 2 * cols], U8, name=name, align_bytes=64)

        def plane_tile(name, cols=NB):
            return keep.tile([P, G, cols], U8, name=name, align_bytes=64)

        def load_codes(tile, words, g0, g1, c0):
            width = tile.shape[2]
            nc.sync.dma_start(
                out=tile[:, g0:g1, :].bitcast(I32),
                in_=words[g0:g1, :, c0 : c0 + width].rearrange("g p c -> p g c").bitcast(I32),
            )

        def load_q_scales(pair, r):
            nc.sync.dma_start(
                out=q_planes[pair][r:P:32, :, :].bitcast(I32),
                in_=wq_scales[:, r:16:4, 2 * NB * pair : 2 * NB * (pair + 1)].rearrange("g q n -> q g n").bitcast(I32),
            )

        def load_q_codes(pair, g0):
            load_codes(q_codes[pair], wq_words, g0, g0 + 2, 4 * NB * pair)

        def load_scales(plane, scales, g0, g1, c0):
            for quad in range(4):
                nc.sync.dma_start(
                    out=plane[32 * quad : 32 * quad + 4, g0:g1, :].bitcast(I32),
                    in_=scales[g0:g1, 4 * quad : 4 * quad + 4, c0 : c0 + NB]
                    .rearrange("g r n -> r g n")
                    .bitcast(I32),
                )

        def zero(engine, plane, g0, g1):
            engine.memset(plane[:, g0:g1, :].rearrange("p g n -> p (g n)").bitcast(I32), 0)

        x_codes = codes_tile("x_codes")
        k_codes = codes_tile("k_codes")
        v_codes = codes_tile("v_codes")
        q_codes = [codes_tile(f"q_codes{i}", 2 * NB) for i in range(QB // 2)]
        x_plane = plane_tile("x_plane")
        k_plane = plane_tile("k_plane")
        v_plane = plane_tile("v_plane")
        q_planes = [plane_tile(f"q_plane{i}", 2 * NB) for i in range(QB // 2)]

        zero(nc.vector, x_plane, 0, G2)
        zero(nc.gpsimd, k_plane, 0, G2)
        dummy = keep.tile([P, NB], BF16, name="dummy")
        nc.vector.memset(dummy[:], 0.0)
        zero(nc.vector, x_plane, G2, G)
        zero(nc.gpsimd, v_plane, 0, G)
        zero(nc.gpsimd, k_plane, G2, G)
        pos = keep.tile([P, TB], F32, name="pos")
        nc.gpsimd.iota(
            pos[:], pattern=[[P, TB]], base=0, channel_multiplier=1, allow_small_or_imprecise_dtypes=True
        )
        for plane in q_planes:
            zero(nc.gpsimd, plane, 0, G)

        load_codes(x_codes, x_words, 0, 1, 0)
        load_codes(k_codes, wk_words, 0, 1, 0)
        load_scales(x_plane, x_scales, 0, G2, 0)
        load_scales(k_plane, wk_scales, 0, G2, 0)
        for g in range(1, G2):
            load_codes(x_codes, x_words, g, g + 1, 0)
            load_codes(k_codes, wk_words, g, g + 1, 0)
        load_scales(v_plane, wv_scales, 0, G, 0)
        load_codes(v_codes, wv_words, 0, G2, 0)
        load_q_scales(0, 0)
        load_codes(x_codes, x_words, G2, G, 0)
        load_codes(k_codes, wk_words, G2, G, 0)
        load_scales(x_plane, x_scales, G2, G, 0)
        load_q_scales(0, 1)
        load_scales(k_plane, wk_scales, G2, G, 0)
        load_codes(v_codes, wv_words, G2, G, 0)
        load_q_scales(0, 2)
        load_q_codes(0, 0)
        load_q_codes(0, 2)
        load_q_scales(0, 3)
        load_q_codes(0, 4)
        for i in range(3):
            load_q_scales(1, i)
            load_q_codes(1, 2 * i)
        load_q_scales(1, 3)

        freq = keep.tile([P, HALF], F32, name="freq")
        one = keep.tile([P, 1], F32, name="one")
        warm = keep.tile([P, 1], F32, name="warm")
        nc.vector.memset(one[:], 1.0)
        nc.scalar.activation(out=warm[:], in_=one[:], func=ACT.Sin)
        nc.vector.tensor_scalar(
            out=freq[:, 0:1], in0=one[:], scalar1=1.0 / (2.0 * math.pi), scalar2=None, op0=ALU.mult
        )
        width = 1
        while width < HALF:
            nc.vector.tensor_scalar(
                out=freq[:, width : 2 * width],
                in0=freq[:, 0:width],
                scalar1=THETA ** (-width / HALF),
                scalar2=None,
                op0=ALU.mult,
            )
            width *= 2
        turns = keep.tile([P, 2, TB, HALF], F32, name="turns")
        whole = keep.tile([P, 2, TB, HALF], I32, name="whole")
        part = keep.tile([P, 2, TB, HALF], F32, name="part")
        for b in range(TB):
            nc.vector.tensor_scalar(
                out=turns[:, 0, b, :], in0=freq[:], scalar1=pos[:, b : b + 1], scalar2=None, op0=ALU.mult
            )
        nc.vector.tensor_scalar(
            out=turns[:, 1, :, :], in0=turns[:, 0, :, :], scalar1=0.25, scalar2=None, op0=ALU.add
        )
        nc.vector.tensor_copy(out=whole[:], in_=turns[:])
        nc.vector.tensor_tensor(out=part[:], in0=turns[:], in1=whole[:], op=ALU.subtract)
        cos = keep.tile([P, TB, HALF], F32, name="cos")
        sin = keep.tile([P, TB, 2, HALF], F32, name="sin")
        nc.scalar.activation(out=cos[:], in_=part[:, 1, :, :], func=ACT.Sin, scale=2.0 * math.pi)
        nc.scalar.activation(out=sin[:, :, 0, :], in_=part[:, 0, :, :], func=ACT.Sin, scale=-2.0 * math.pi)
        nc.scalar.activation(out=sin[:, :, 1, :], in_=part[:, 0, :, :], func=ACT.Sin, scale=2.0 * math.pi)

        def multiply(acc, tb, g, codes, plane, c0, cols):
            nc.tensor.matmul_mx(
                out=acc,
                lhsT=x_codes[:, g, 2 * P * tb : 2 * P * (tb + 1)].bitcast(FP4X4),
                lhsT_scale=x_plane[:, g, P * tb : P * (tb + 1)],
                rhs=codes[:, g, 2 * c0 : 2 * (c0 + cols)].bitcast(FP4X4),
                rhs_scale=plane[:, g, c0 : c0 + cols],
                start=(g == 0),
                stop=(g == G - 1),
            )

        def heads(out, h0, h1, tb):
            return out[0, h0:h1, P * tb : P * (tb + 1), :].rearrange("h p j -> p h j")

        waiting = []

        def add_and_store(engine, res, rot, dst):
            engine.tensor_tensor(out=res, in0=res, in1=rot, op=ALU.add)
            nc.sync.dma_start(out=dst, in_=res.rearrange("p (h j) -> p h j", j=HD))

        def flush():
            while len(waiting) > 0:
                add_and_store(nc.vector, *waiting[0])
                waiting.remove(waiting[0])

        def rope(acc, tb, out, h0, n_heads, on_gpsimd):
            cols = n_heads * HD
            res_tile = work.tile([P, NB], F32, name="res", bufs=8)
            rot_tile = work.tile([P, NB], F32, name="rot")
            res = res_tile[:, 0:cols]
            rot = rot_tile[:, 0:cols]
            nc.vector.tensor_tensor(
                out=res.rearrange("p (h j) -> p h j", j=HALF),
                in0=acc.rearrange("p (h j) -> p h j", j=HALF),
                in1=cos[:, tb, :].unsqueeze(1).to_broadcast([P, 2 * n_heads, HALF]),
                op=ALU.mult,
            )
            flush()
            nc.vector.tensor_tensor(
                out=rot.rearrange("p (h s j) -> p h s j", s=2, j=HALF),
                in0=acc.rearrange("p (h s j) -> p h s j", s=2, j=HALF)[:, :, ::-1, :],
                in1=sin[:, tb, :, :].unsqueeze(1).to_broadcast([P, n_heads, 2, HALF]),
                op=ALU.mult,
            )
            dst = heads(out, h0, h0 + n_heads, tb)
            if on_gpsimd:
                add_and_store(nc.gpsimd, res, rot, dst)
            else:
                waiting.append((res, rot, dst))

        scratch = psum.tile([P, NB], F32, name="acc")
        for i in range(10):
            nc.tensor.matmul(scratch[:], lhsT=dummy[:, 0:P], rhs=dummy[:], start=True, stop=True)

        k_accs = [psum.tile([P, NB], F32, name="acc") for b in range(TB)]
        v_accs = [psum.tile([P, NB], F32, name="acc") for b in range(TB - 1)]
        k_group = (k_accs, k_codes, k_plane)
        v_group = (v_accs, v_codes, v_plane)
        for g0, groups in ((0, (k_group, v_group)), (G2, (k_group, v_group))):
            for accs, codes, plane in groups:
                for g in range(g0, g0 + G2):
                    for tb in range(len(accs)):
                        multiply(accs[tb][:], tb, g, codes, plane, 0, NB)
        for tb in range(TB):
            rope(k_accs[tb][:], tb, out_k, 0, HPB, True)
        for tb in range(TB - 1):
            res = work.tile([P, NB], F32, name="res", bufs=8)
            nc.scalar.copy(out=res[:], in_=v_accs[tb][:])
            nc.sync.dma_start(out=heads(out_v, 0, HPB, tb), in_=res[:].rearrange("p (h j) -> p h j", j=HD))

        for n in range(QB):
            for tb in range(TB):
                parts = 2 if n == QB - 1 and tb == TB - 1 else 1
                cols = NB // parts
                for i in range(parts):
                    acc = psum.tile([P, NB], F32, name="acc")
                    for g in range(G):
                        multiply(acc[:, 0:cols], tb, g, q_codes[n // 2], q_planes[n // 2], NB * (n % 2) + cols * i, cols)
                    h0 = HPB * n + cols // HD * i
                    rope(acc[:, 0:cols], tb, out_q, h0, cols // HD, tb < TB - 1)
        flush()

        tb = TB - 1
        for half in range(2):
            cols = NB // 2
            acc = psum.tile([P, NB], F32, name="acc")
            for g in range(G):
                multiply(acc[:, 0:cols], tb, g, v_codes, v_plane, cols * half, cols)
            res = work.tile([P, NB], F32, name="res", bufs=8)
            nc.scalar.copy(out=res[:, 0:cols], in_=acc[:, 0:cols])
            nc.scalar.dma_start(
                out=heads(out_v, half * HPB // 2, (half + 1) * HPB // 2, tb),
                in_=res[:, 0:cols].rearrange("p (h j) -> p h j", j=HD),
            )
